import numpy as np
import ml_dtypes


def mxq(x, axis, fmt="e4m3"):
    dtype, down = {"e4m3": (ml_dtypes.float8_e4m3fn, 7), "e5m2": (ml_dtypes.float8_e5m2, 14)}[fmt]
    v = np.moveaxis(np.asarray(x, np.float32).astype(ml_dtypes.bfloat16).astype(np.float64), axis, -1)
    blocks = v.reshape(v.shape[:-1] + (-1, 32))
    amax = np.abs(blocks).max(-1, keepdims=True)
    byte = np.maximum(np.where(amax > 0, np.frexp(amax)[1] - 1 + 127, 0) - down, 1)
    scale = np.exp2(byte - 127.0)
    codes = (blocks / scale).astype(np.float32).astype(dtype).astype(np.float64)
    return np.moveaxis((codes * scale).reshape(v.shape), -1, axis)


WIDE = False


def mx_kscale(k):
    if not WIDE:
        return np.ones(k)
    levels = np.array([10, -10, 5, -5, 0])
    if k % 512:
        return np.exp2(np.random.permutation(np.resize(levels, k // 32))).repeat(32)
    a = np.empty((k // 512, 16))
    for p in range(k // 512):
        a[p, :8] = np.random.permutation(np.resize(levels, 8))
        for g in range(8):
            far = levels[np.abs(levels - a[p, g]) >= 10]
            a[p, g + 8] = far[np.random.randint(len(far))]
    return np.exp2(a.ravel()).repeat(32)


BF16 = ml_dtypes.bfloat16


def bf(x):
    return np.asarray(x, np.float32).astype(BF16)


def f64(x):
    return np.asarray(x).astype(np.float64)


S, E, HQ, HK, D, C = 8192, 1024, 4, 4, 32, 512


def rotate_half(t):
    t1, t2 = np.split(t, 2, axis=-1)
    return np.concatenate([-t2, t1], axis=-1)


def setup_inputs():
    s = mx_kscale(E)
    theta = np.random.uniform(0.0, 2.0 * np.pi, (S, D // 2))
    theta = np.concatenate([theta, theta], axis=-1)
    return {"x": bf(np.random.standard_normal((S, E)) * s),
            "w_q": bf(np.random.standard_normal((HQ * D, E)) * 1.4 / np.sqrt(E) / s[None, :]),
            "w_k": bf(np.random.standard_normal((HK * D, E)) * 1.4 / np.sqrt(E) / s[None, :]),
            "w_v": bf(np.random.standard_normal((HK * D, E)) / np.sqrt(E) / s[None, :]),
            "cos_tab": bf(np.cos(theta)), "sin_tab": bf(np.sin(theta))}


def reference(x, w_q, w_k, w_v, cos_tab, sin_tab):
    xq = mxq(f64(x), 1, "e4m3")
    q = (xq @ mxq(f64(w_q), 1, "e4m3").T).reshape(S, HQ, D)
    k = (xq @ mxq(f64(w_k), 1, "e4m3").T).reshape(S, HK, D)
    v = (xq @ mxq(f64(w_v), 1, "e4m3").T).reshape(S, HK, D)
    c = f64(cos_tab).reshape(S, 1, D)
    sn = f64(sin_tab).reshape(S, 1, D)
    q_rot = q * c + rotate_half(q) * sn
    k_rot = k * c + rotate_half(k) * sn
    return q_rot, k_rot, v

@@ -1,0 +1,224 @@
+from contextlib import ExitStack
+
+import concourse.mybir as mybir
+from concourse.masks import make_identity
+
+F32 = mybir.dt.float32
+BF16 = mybir.dt.bfloat16
+U32 = mybir.dt.uint32
+U8 = mybir.dt.uint8
+FP8X4 = mybir.dt.float8_e4m3fn_x4
+MULT = mybir.AluOpType.mult
+ADD = mybir.AluOpType.add
+
+P = 128
+ROWS = 8192
+K = 1024
+HEADS = 4
+HEAD_DIM = 32
+HALF = HEAD_DIM // 2
+FEATURES = HEADS * HEAD_DIM
+QK = 2 * FEATURES
+QK_HEADS = 2 * HEADS
+K_PASS = 4 * P
+PASSES = K // K_PASS
+K_WORDS = K // 2
+WORD_BLOCKS = K_WORDS // P
+TILES = ROWS // P
+PAIR = 2
+PAIRS = TILES // PAIR
+CHUNK = 4
+CHUNKS = TILES // CHUNK
+X_AHEAD = 6
+TABLE_CHUNKS = 4
+
+FLOPS = 2 * ROWS * K * 3 * FEATURES
+
+
+def transpose_words(nc, psum, words, identity, copy, grouped_words):
+    flipped = psum.tile([P, WORD_BLOCKS, P], F32, tag="flipped")
+    for j in range(WORD_BLOCKS):
+        g, u = divmod(j, 2)
+        nc.tensor.transpose(flipped[:, j, :], words[:, 2 * P * g + u : 2 * P * (g + 1) : 2], identity)
+    copy(out=grouped_words, in_=flipped[:].rearrange("p (g u) r -> p g r u", u=2))
+
+
+def tile_groupedqueryattention_pa_t_kernel(
+    tc, x, w_q, w_k, w_v, cos_tab, sin_tab, out_0, out_1, out_2
+):
+    nc = tc.nc
+    x_tiles = x.rearrange("(p n) k -> p n k", n=TILES)
+    cos_tiles = cos_tab.rearrange("(p n) d -> p n d", n=TILES)
+    sin_tiles = sin_tab.rearrange("(p n) d -> p n d", n=TILES)
+    out_tiles = [o.rearrange("(p n) h d -> p n (h d)", n=TILES) for o in (out_0, out_1, out_2)]
+
+    with ExitStack() as ctx:
+        ctx.enter_context(tc.manual_schedule())
+        const = ctx.enter_context(tc.tile_pool(name="const", bufs=1))
+        x_pool = ctx.enter_context(tc.tile_pool(name="x_pool", bufs=X_AHEAD))
+        mx_pool = ctx.enter_context(tc.tile_pool(name="mx_pool", bufs=2))
+        work_pool = ctx.enter_context(tc.tile_pool(name="work_pool", bufs=3))
+        out_pool = ctx.enter_context(tc.tile_pool(name="out_pool", bufs=4))
+        psum_flip = ctx.enter_context(tc.psum_pool(name="psum_flip", bufs=3))
+        psum_acc = ctx.enter_context(tc.psum_pool(name="psum_acc", bufs=3))
+
+        x_of = {}
+        grouped_of = {}
+        codes_of = {}
+        sums_of = {}
+        qk_out_of = {}
+        v_out_of = {}
+
+        cos_sb = const.tile([P, TILES, HEAD_DIM], BF16)
+        sin_sb = const.tile([P, TILES, HEAD_DIM], BF16)
+
+        def load(c):
+            x_sb = x_pool.tile([P, CHUNK, K], BF16, tag="x_sb")
+            step = 1 if c == 0 else CHUNK
+            for t in range(0, CHUNK, step):
+                nc.sync.dma_start(
+                    out=x_sb[:, t : t + step, :],
+                    in_=x_tiles[:, c * CHUNK + t : c * CHUNK + t + step, :],
+                )
+            x_of[c] = x_sb
+            if c % TABLE_CHUNKS == 0:
+                piece = slice(c * CHUNK, (c + TABLE_CHUNKS) * CHUNK)
+                nc.sync.dma_start(out=cos_sb[:, piece, :], in_=cos_tiles[:, piece, :])
+                nc.sync.dma_start(out=sin_sb[:, piece, :], in_=sin_tiles[:, piece, :])
+
+        w_sb = const.tile([P, 3 * K], BF16)
+        for o, w in enumerate((w_q, w_k, w_v)):
+            nc.sync.dma_start(out=w_sb[:, o * K : (o + 1) * K], in_=w)
+        for c in range(X_AHEAD):
+            load(c)
+
+        identity = const.tile([P, P], F32)
+        make_identity(nc, identity[:])
+
+        w_grouped = const.tile([P, 3 * K], BF16, align_bytes=64)
+        w_codes = const.tile([P, PASSES, 3 * FEATURES], U32, align_bytes=64)
+        w_scales = const.tile([P, PASSES, 3 * FEATURES], U8, align_bytes=64)
+        w_words = w_sb[:].bitcast(F32)
+        w_grouped_words = w_grouped[:].bitcast(F32).rearrange(
+            "p (g o r u) -> p g o r u", g=PASSES, o=3, u=2
+        )
+        for o in range(3):
+            transpose_words(
+                nc,
+                psum_flip,
+                w_words[:, o * K_WORDS : (o + 1) * K_WORDS],
+                identity[:],
+                nc.vector.tensor_copy,
+                w_grouped_words[:, :, o],
+            )
+        for g in range(PASSES):
+            for o in range(3):
+                features = slice(o * FEATURES, (o + 1) * FEATURES)
+                values = slice((g * 3 + o) * 4 * FEATURES, (g * 3 + o + 1) * 4 * FEATURES)
+                nc.vector.quantize_mx(
+                    out=w_codes[:, g, features].bitcast(FP8X4),
+                    scales=w_scales[:, g, features],
+                    in_=w_grouped[:, values],
+                )
+
+        def transpose(i):
+            c, first = divmod(i * PAIR, CHUNK)
+            words = x_of[c][:].rearrange("p t k -> p (t k)").bitcast(F32)
+            grouped = mx_pool.tile([P, PAIR * K], BF16, tag="grouped", align_bytes=64)
+            grouped_words = grouped[:].bitcast(F32).rearrange(
+                "p (t g r u) -> p t g r u", t=PAIR, g=PASSES, u=2
+            )
+            for t in range(PAIR):
+                transpose_words(
+                    nc,
+                    psum_flip,
+                    words[:, (first + t) * K_WORDS : (first + t + 1) * K_WORDS],
+                    identity[:],
+                    nc.scalar.copy,
+                    grouped_words[:, t],
+                )
+            grouped_of[i] = grouped
+
+        def quantise(i):
+            codes = mx_pool.tile([P, PAIR, PASSES, P], U32, tag="codes", align_bytes=64)
+            scales = mx_pool.tile([P, PAIR, PASSES, P], U8, tag="scales", align_bytes=64)
+            nc.vector.quantize_mx(
+                out=codes[:].rearrange("p t g r -> p (t g r)").bitcast(FP8X4),
+                scales=scales[:].rearrange("p t g r -> p (t g r)"),
+                in_=grouped_of[i][:],
+            )
+            codes_of[i] = (codes, scales)
+
+        def project(i):
+            codes, scales = codes_of[i]
+            qk_sum = psum_acc.tile([P, PAIR, QK], F32, tag="qk_sum")
+            v_sum = psum_acc.tile([P, PAIR, FEATURES], F32, tag="v_sum", bufs=2)
+            for t in range(PAIR):
+                for acc, features in ((qk_sum, slice(0, QK)), (v_sum, slice(QK, QK + FEATURES))):
+                    for g in range(PASSES):
+                        nc.tensor.matmul_mx(
+                            out=acc[:, t, :],
+                            lhsT=codes[:, t, g, :].bitcast(FP8X4),
+                            lhsT_scale=scales[:, t, g, :],
+                            rhs=w_codes[:, g, features].bitcast(FP8X4),
+                            rhs_scale=w_scales[:, g, features],
+                            start=(g == 0),
+                            stop=(g == PASSES - 1),
+                        )
+            sums_of[i] = qk_sum
+            c, first = divmod(i * PAIR, CHUNK)
+            if first == 0:
+                v_out = out_pool.tile([P, CHUNK, FEATURES], F32, tag="v_out")
+                v_out_of[c] = v_out
+            nc.scalar.copy(out=v_out_of[c][:, first : first + PAIR, :], in_=v_sum[:])
+
+        def rotate(i):
+            c, first = divmod(i * PAIR, CHUNK)
+            if first == 0 and c % TABLE_CHUNKS == 0:
+                piece = slice(c * CHUNK, (c + TABLE_CHUNKS) * CHUNK)
+                nc.vector.tensor_scalar_mul(
+                    out=sin_sb[:, piece, 0:HALF], in0=sin_sb[:, piece, 0:HALF], scalar1=-1.0
+                )
+            tiles = slice(i * PAIR, (i + 1) * PAIR)
+            by_head = [P, PAIR, QK_HEADS, HEAD_DIM]
+            half_by_head = [P, PAIR, QK_HEADS, HALF]
+            cos = cos_sb[:, tiles, :].unsqueeze(2).to_broadcast(by_head)
+            sin_low = sin_sb[:, tiles, 0:HALF].unsqueeze(2).to_broadcast(half_by_head)
+            sin_high = sin_sb[:, tiles, HALF:HEAD_DIM].unsqueeze(2).to_broadcast(half_by_head)
+            sums = sums_of[i][:].rearrange("p t (h d) -> p t h d", d=HEAD_DIM)
+            straight = work_pool.tile(by_head, F32, tag="straight")
+            crossed = work_pool.tile(by_head, F32, tag="crossed")
+            nc.vector.tensor_tensor(out=straight[:], in0=sums, in1=cos, op=MULT)
+            nc.vector.tensor_tensor(
+                out=crossed[:, :, :, 0:HALF], in0=sums[:, :, :, HALF:HEAD_DIM], in1=sin_low, op=MULT
+            )
+            nc.vector.tensor_tensor(
+                out=crossed[:, :, :, HALF:HEAD_DIM], in0=sums[:, :, :, 0:HALF], in1=sin_high, op=MULT
+            )
+            if first == 0:
+                qk_out = out_pool.tile([P, 2, CHUNK, FEATURES], F32, tag="qk_out")
+                qk_out_of[c] = qk_out
+            nc.gpsimd.tensor_tensor(
+                out=qk_out_of[c][:, :, first : first + PAIR, :],
+                in0=straight[:].rearrange("p t (o h) d -> p o t (h d)", o=2),
+                in1=crossed[:].rearrange("p t (o h) d -> p o t (h d)", o=2),
+                op=ADD,
+            )
+            if first + PAIR == CHUNK:
+                chunk_tiles = slice(c * CHUNK, (c + 1) * CHUNK)
+                for o in range(2):
+                    nc.sync.dma_start(out=out_tiles[o][:, chunk_tiles, :], in_=qk_out_of[c][:, o])
+                nc.sync.dma_start(out=out_tiles[2][:, chunk_tiles, :], in_=v_out_of[c][:])
+
+        for i in range(-3, PAIRS):
+            c, first = divmod(i * PAIR, CHUNK)
+            if first == 0 and 0 <= c and c + X_AHEAD < CHUNKS:
+                load(c + X_AHEAD)
+            if 0 <= i + 2 < PAIRS:
+                quantise(i + 2)
+            if i + 3 < PAIRS:
+                transpose(i + 3)
+            if 0 <= i + 1 < PAIRS:
+                project(i + 1)
+            if 0 <= i:
+                rotate(i)

@@ -31,6 +31,7 @@ CHUNK = 4
 CHUNKS = TILES // CHUNK
 X_AHEAD = 6
 TABLE_CHUNKS = 4
+TILEWISE_CHUNKS = 2
 
 FLOPS = 2 * ROWS * K * 3 * FEATURES
 
@@ -74,15 +75,15 @@ def tile_groupedqueryattention_pa_t_kernel(
 
         def load(c):
             x_sb = x_pool.tile([P, CHUNK, K], BF16, tag="x_sb")
-            step = 1 if c == 0 else CHUNK
+            step = 1 if c < TILEWISE_CHUNKS else CHUNK
             for t in range(0, CHUNK, step):
                 nc.sync.dma_start(
                     out=x_sb[:, t : t + step, :],
                     in_=x_tiles[:, c * CHUNK + t : c * CHUNK + t + step, :],
                 )
             x_of[c] = x_sb
-            if c % TABLE_CHUNKS == 0:
-                piece = slice(c * CHUNK, (c + TABLE_CHUNKS) * CHUNK)
+            if c % TABLE_CHUNKS == TILEWISE_CHUNKS - 1:
+                piece = slice((c - c % TABLE_CHUNKS) * CHUNK, (c - c % TABLE_CHUNKS + TABLE_CHUNKS) * CHUNK)
                 nc.sync.dma_start(out=cos_sb[:, piece, :], in_=cos_tiles[:, piece, :])
                 nc.sync.dma_start(out=sin_sb[:, piece, :], in_=sin_tiles[:, piece, :])
 
@@ -198,17 +199,34 @@ def tile_groupedqueryattention_pa_t_kernel(
             if first == 0:
                 qk_out = out_pool.tile([P, 2, CHUNK, FEATURES], F32, tag="qk_out")
                 qk_out_of[c] = qk_out
-            nc.gpsimd.tensor_tensor(
-                out=qk_out_of[c][:, :, first : first + PAIR, :],
-                in0=straight[:].rearrange("p t (o h) d -> p o t (h d)", o=2),
-                in1=crossed[:].rearrange("p t (o h) d -> p o t (h d)", o=2),
-                op=ADD,
-            )
-            if first + PAIR == CHUNK:
-                chunk_tiles = slice(c * CHUNK, (c + 1) * CHUNK)
+            if i < PAIRS - 1:
+                nc.gpsimd.tensor_tensor(
+                    out=qk_out_of[c][:, :, first : first + PAIR, :],
+                    in0=straight[:].rearrange("p t (o h) d -> p o t (h d)", o=2),
+                    in1=crossed[:].rearrange("p t (o h) d -> p o t (h d)", o=2),
+                    op=ADD,
+                )
+            else:
+                last_out = out_pool.tile([P, PAIR, 2, FEATURES], F32, tag="last_out", bufs=1)
+                for half in (slice(0, HALF), slice(HALF, HEAD_DIM)):
+                    nc.vector.tensor_tensor(
+                        out=last_out[:].rearrange("p t o (h d) -> p (t o h) d", d=HEAD_DIM)[:, :, half],
+                        in0=straight[:].rearrange("p t h d -> p (t h) d")[:, :, half],
+                        in1=crossed[:].rearrange("p t h d -> p (t h) d")[:, :, half],
+                        op=ADD,
+                    )
+            if c == CHUNKS - 1:
+                stored = slice(first, first + PAIR)
+            elif first + PAIR == CHUNK:
+                stored = slice(0, CHUNK)
+            else:
+                stored = None
+            if stored is not None:
+                tiles_out = slice(c * CHUNK + stored.start, c * CHUNK + stored.stop)
+                nc.sync.dma_start(out=out_tiles[2][:, tiles_out, :], in_=v_out_of[c][:, stored, :])
                 for o in range(2):
-                    nc.sync.dma_start(out=out_tiles[o][:, chunk_tiles, :], in_=qk_out_of[c][:, o])
-                nc.sync.dma_start(out=out_tiles[2][:, chunk_tiles, :], in_=v_out_of[c][:])
+                    rotated = qk_out_of[c][:, o, stored, :] if i < PAIRS - 1 else last_out[:, :, o, :]
+                    nc.sync.dma_start(out=out_tiles[o][:, tiles_out, :], in_=rotated)
 
         for i in range(-3, PAIRS):
             c, first = divmod(i * PAIR, CHUNK)

@@ -182,19 +182,17 @@ def tile_groupedqueryattention_pa_t_kernel(
                 )
             tiles = slice(i * PAIR, (i + 1) * PAIR)
             by_head = [P, PAIR, QK_HEADS, HEAD_DIM]
-            half_by_head = [P, PAIR, QK_HEADS, HALF]
             cos = cos_sb[:, tiles, :].unsqueeze(2).to_broadcast(by_head)
-            sin_low = sin_sb[:, tiles, 0:HALF].unsqueeze(2).to_broadcast(half_by_head)
-            sin_high = sin_sb[:, tiles, HALF:HEAD_DIM].unsqueeze(2).to_broadcast(half_by_head)
             sums = sums_of[i][:].rearrange("p t (h d) -> p t h d", d=HEAD_DIM)
             straight = work_pool.tile(by_head, F32, tag="straight")
             crossed = work_pool.tile(by_head, F32, tag="crossed")
             nc.vector.tensor_tensor(out=straight[:], in0=sums, in1=cos, op=MULT)
+            by_half = [P, PAIR, QK_HEADS, 2, HALF]
             nc.vector.tensor_tensor(
-                out=crossed[:, :, :, 0:HALF], in0=sums[:, :, :, HALF:HEAD_DIM], in1=sin_low, op=MULT
-            )
-            nc.vector.tensor_tensor(
-                out=crossed[:, :, :, HALF:HEAD_DIM], in0=sums[:, :, :, 0:HALF], in1=sin_high, op=MULT
+                out=crossed[:].rearrange("p t h (s d) -> p t h s d", s=2),
+                in0=sums.rearrange("p t h (s d) -> p t h s d", s=2)[:, :, :, ::-1, :],
+                in1=sin_sb[:, tiles, :].rearrange("p t (s d) -> p t s d", s=2).unsqueeze(2).to_broadcast(by_half),
+                op=MULT,
             )
             if first == 0:
                 qk_out = out_pool.tile([P, 2, CHUNK, FEATURES], F32, tag="qk_out")

from contextlib import ExitStack

import concourse.mybir as mybir
from concourse.masks import make_identity

F32 = mybir.dt.float32
BF16 = mybir.dt.bfloat16
U32 = mybir.dt.uint32
U8 = mybir.dt.uint8
FP8X4 = mybir.dt.float8_e4m3fn_x4
MULT = mybir.AluOpType.mult
ADD = mybir.AluOpType.add

P = 128
ROWS = 8192
K = 1024
HEADS = 4
HEAD_DIM = 32
HALF = HEAD_DIM // 2
FEATURES = HEADS * HEAD_DIM
QK = 2 * FEATURES
QK_HEADS = 2 * HEADS
K_PASS = 4 * P
PASSES = K // K_PASS
K_WORDS = K // 2
WORD_BLOCKS = K_WORDS // P
TILES = ROWS // P
PAIR = 2
PAIRS = TILES // PAIR
CHUNK = 4
CHUNKS = TILES // CHUNK
X_AHEAD = 6
TABLE_CHUNKS = 4
TILEWISE_CHUNKS = 2

FLOPS = 2 * ROWS * K * 3 * FEATURES


def transpose_words(nc, psum, words, identity, copy, grouped_words):
    flipped = psum.tile([P, WORD_BLOCKS, P], F32, tag="flipped")
    for j in range(WORD_BLOCKS):
        g, u = divmod(j, 2)
        nc.tensor.transpose(flipped[:, j, :], words[:, 2 * P * g + u : 2 * P * (g + 1) : 2], identity)
    copy(out=grouped_words, in_=flipped[:].rearrange("p (g u) r -> p g r u", u=2))


def tile_groupedqueryattention_pa_t_kernel(
    tc, x, w_q, w_k, w_v, cos_tab, sin_tab, out_0, out_1, out_2
):
    nc = tc.nc
    x_tiles = x.rearrange("(p n) k -> p n k", n=TILES)
    cos_tiles = cos_tab.rearrange("(p n) d -> p n d", n=TILES)
    sin_tiles = sin_tab.rearrange("(p n) d -> p n d", n=TILES)
    out_tiles = [o.rearrange("(p n) h d -> p n (h d)", n=TILES) for o in (out_0, out_1, out_2)]

    with ExitStack() as ctx:
        ctx.enter_context(tc.manual_schedule())
        const = ctx.enter_context(tc.tile_pool(name="const", bufs=1))
        x_pool = ctx.enter_context(tc.tile_pool(name="x_pool", bufs=X_AHEAD))
        mx_pool = ctx.enter_context(tc.tile_pool(name="mx_pool", bufs=2))
        work_pool = ctx.enter_context(tc.tile_pool(name="work_pool", bufs=3))
        out_pool = ctx.enter_context(tc.tile_pool(name="out_pool", bufs=4))
        psum_flip = ctx.enter_context(tc.psum_pool(name="psum_flip", bufs=3))
        psum_acc = ctx.enter_context(tc.psum_pool(name="psum_acc", bufs=3))

        x_of = {}
        grouped_of = {}
        codes_of = {}
        sums_of = {}
        qk_out_of = {}
        v_out_of = {}

        cos_sb = const.tile([P, TILES, HEAD_DIM], BF16)
        sin_sb = const.tile([P, TILES, HEAD_DIM], BF16)

        def load(c):
            x_sb = x_pool.tile([P, CHUNK, K], BF16, tag="x_sb")
            step = 1 if c < TILEWISE_CHUNKS else CHUNK
            for t in range(0, CHUNK, step):
                nc.sync.dma_start(
                    out=x_sb[:, t : t + step, :],
                    in_=x_tiles[:, c * CHUNK + t : c * CHUNK + t + step, :],
                )
            x_of[c] = x_sb
            if c % TABLE_CHUNKS == TILEWISE_CHUNKS - 1:
                piece = slice((c - c % TABLE_CHUNKS) * CHUNK, (c - c % TABLE_CHUNKS + TABLE_CHUNKS) * CHUNK)
                nc.sync.dma_start(out=cos_sb[:, piece, :], in_=cos_tiles[:, piece, :])
                nc.sync.dma_start(out=sin_sb[:, piece, :], in_=sin_tiles[:, piece, :])

        w_sb = const.tile([P, 3 * K], BF16)
        for o, w in enumerate((w_q, w_k, w_v)):
            nc.sync.dma_start(out=w_sb[:, o * K : (o + 1) * K], in_=w)
        for c in range(X_AHEAD):
            load(c)

        identity = const.tile([P, P], F32)
        make_identity(nc, identity[:])

        w_grouped = const.tile([P, 3 * K], BF16, align_bytes=64)
        w_codes = const.tile([P, PASSES, 3 * FEATURES], U32, align_bytes=64)
        w_scales = const.tile([P, PASSES, 3 * FEATURES], U8, align_bytes=64)
        w_words = w_sb[:].bitcast(F32)
        w_grouped_words = w_grouped[:].bitcast(F32).rearrange(
            "p (g o r u) -> p g o r u", g=PASSES, o=3, u=2
        )
        for o in range(3):
            transpose_words(
                nc,
                psum_flip,
                w_words[:, o * K_WORDS : (o + 1) * K_WORDS],
                identity[:],
                nc.vector.tensor_copy,
                w_grouped_words[:, :, o],
            )
        for g in range(PASSES):
            for o in range(3):
                features = slice(o * FEATURES, (o + 1) * FEATURES)
                values = slice((g * 3 + o) * 4 * FEATURES, (g * 3 + o + 1) * 4 * FEATURES)
                nc.vector.quantize_mx(
                    out=w_codes[:, g, features].bitcast(FP8X4),
                    scales=w_scales[:, g, features],
                    in_=w_grouped[:, values],
                )

        def transpose(i):
            c, first = divmod(i * PAIR, CHUNK)
            words = x_of[c][:].rearrange("p t k -> p (t k)").bitcast(F32)
            grouped = mx_pool.tile([P, PAIR * K], BF16, tag="grouped", align_bytes=64)
            grouped_words = grouped[:].bitcast(F32).rearrange(
                "p (t g r u) -> p t g r u", t=PAIR, g=PASSES, u=2
            )
            for t in range(PAIR):
                transpose_words(
                    nc,
                    psum_flip,
                    words[:, (first + t) * K_WORDS : (first + t + 1) * K_WORDS],
                    identity[:],
                    nc.scalar.copy,
                    grouped_words[:, t],
                )
            grouped_of[i] = grouped

        def quantise(i):
            codes = mx_pool.tile([P, PAIR, PASSES, P], U32, tag="codes", align_bytes=64)
            scales = mx_pool.tile([P, PAIR, PASSES, P], U8, tag="scales", align_bytes=64)
            nc.vector.quantize_mx(
                out=codes[:].rearrange("p t g r -> p (t g r)").bitcast(FP8X4),
                scales=scales[:].rearrange("p t g r -> p (t g r)"),
                in_=grouped_of[i][:],
            )
            codes_of[i] = (codes, scales)

        def project(i):
            codes, scales = codes_of[i]
            qk_sum = psum_acc.tile([P, PAIR, QK], F32, tag="qk_sum")
            v_sum = psum_acc.tile([P, PAIR, FEATURES], F32, tag="v_sum", bufs=2)
            for t in range(PAIR):
                for acc, features in ((qk_sum, slice(0, QK)), (v_sum, slice(QK, QK + FEATURES))):
                    for g in range(PASSES):
                        nc.tensor.matmul_mx(
                            out=acc[:, t, :],
                            lhsT=codes[:, t, g, :].bitcast(FP8X4),
                            lhsT_scale=scales[:, t, g, :],
                            rhs=w_codes[:, g, features].bitcast(FP8X4),
                            rhs_scale=w_scales[:, g, features],
                            start=(g == 0),
                            stop=(g == PASSES - 1),
                        )
            sums_of[i] = qk_sum
            c, first = divmod(i * PAIR, CHUNK)
            if first == 0:
                v_out = out_pool.tile([P, CHUNK, FEATURES], F32, tag="v_out")
                v_out_of[c] = v_out
            nc.scalar.copy(out=v_out_of[c][:, first : first + PAIR, :], in_=v_sum[:])

        def rotate(i):
            c, first = divmod(i * PAIR, CHUNK)
            if first == 0 and c % TABLE_CHUNKS == 0:
                piece = slice(c * CHUNK, (c + TABLE_CHUNKS) * CHUNK)
                nc.vector.tensor_scalar_mul(
                    out=sin_sb[:, piece, 0:HALF], in0=sin_sb[:, piece, 0:HALF], scalar1=-1.0
                )
            tiles = slice(i * PAIR, (i + 1) * PAIR)
            by_head = [P, PAIR, QK_HEADS, HEAD_DIM]
            cos = cos_sb[:, tiles, :].unsqueeze(2).to_broadcast(by_head)
            sums = sums_of[i][:].rearrange("p t (h d) -> p t h d", d=HEAD_DIM)
            straight = work_pool.tile(by_head, F32, tag="straight")
            crossed = work_pool.tile(by_head, F32, tag="crossed")
            nc.vector.tensor_tensor(out=straight[:], in0=sums, in1=cos, op=MULT)
            by_half = [P, PAIR, QK_HEADS, 2, HALF]
            nc.vector.tensor_tensor(
                out=crossed[:].rearrange("p t h (s d) -> p t h s d", s=2),
                in0=sums.rearrange("p t h (s d) -> p t h s d", s=2)[:, :, :, ::-1, :],
                in1=sin_sb[:, tiles, :].rearrange("p t (s d) -> p t s d", s=2).unsqueeze(2).to_broadcast(by_half),
                op=MULT,
            )
            if first == 0:
                qk_out = out_pool.tile([P, 2, CHUNK, FEATURES], F32, tag="qk_out")
                qk_out_of[c] = qk_out
            if i < PAIRS - 1:
                nc.gpsimd.tensor_tensor(
                    out=qk_out_of[c][:, :, first : first + PAIR, :],
                    in0=straight[:].rearrange("p t (o h) d -> p o t (h d)", o=2),
                    in1=crossed[:].rearrange("p t (o h) d -> p o t (h d)", o=2),
                    op=ADD,
                )
            else:
                last_out = out_pool.tile([P, PAIR, 2, FEATURES], F32, tag="last_out", bufs=1)
                for half in (slice(0, HALF), slice(HALF, HEAD_DIM)):
                    nc.vector.tensor_tensor(
                        out=last_out[:].rearrange("p t o (h d) -> p (t o h) d", d=HEAD_DIM)[:, :, half],
                        in0=straight[:].rearrange("p t h d -> p (t h) d")[:, :, half],
                        in1=crossed[:].rearrange("p t h d -> p (t h) d")[:, :, half],
                        op=ADD,
                    )
            if c == CHUNKS - 1:
                stored = slice(first, first + PAIR)
            elif first + PAIR == CHUNK:
                stored = slice(0, CHUNK)
            else:
                stored = None
            if stored is not None:
                tiles_out = slice(c * CHUNK + stored.start, c * CHUNK + stored.stop)
                nc.sync.dma_start(out=out_tiles[2][:, tiles_out, :], in_=v_out_of[c][:, stored, :])
                for o in range(2):
                    rotated = qk_out_of[c][:, o, stored, :] if i < PAIRS - 1 else last_out[:, :, o, :]
                    nc.sync.dma_start(out=out_tiles[o][:, tiles_out, :], in_=rotated)

        for i in range(-3, PAIRS):
            c, first = divmod(i * PAIR, CHUNK)
            if first == 0 and 0 <= c and c + X_AHEAD < CHUNKS:
                load(c + X_AHEAD)
            if 0 <= i + 2 < PAIRS:
                quantise(i + 2)
            if i + 3 < PAIRS:
                transpose(i + 3)
            if 0 <= i + 1 < PAIRS:
                project(i + 1)
            if 0 <= i:
                rotate(i)
